import numpy as np
import ml_dtypes


def mxq(x, axis, fmt="e4m3"):
    dtype, down = {"e4m3": (ml_dtypes.float8_e4m3fn, 7), "e5m2": (ml_dtypes.float8_e5m2, 14)}[fmt]
    v = np.moveaxis(np.asarray(x, np.float32).astype(ml_dtypes.bfloat16).astype(np.float64), axis, -1)
    blocks = v.reshape(v.shape[:-1] + (-1, 32))
    amax = np.abs(blocks).max(-1, keepdims=True)
    byte = np.maximum(np.where(amax > 0, np.frexp(amax)[1] - 1 + 127, 0) - down, 1)
    scale = np.exp2(byte - 127.0)
    codes = (blocks / scale).astype(np.float32).astype(dtype).astype(np.float64)
    return np.moveaxis((codes * scale).reshape(v.shape), -1, axis)


WIDE = False


def mx_kscale(k):
    if not WIDE:
        return np.ones(k)
    levels = np.array([10, -10, 5, -5, 0])
    if k % 512:
        return np.exp2(np.random.permutation(np.resize(levels, k // 32))).repeat(32)
    a = np.empty((k // 512, 16))
    for p in range(k // 512):
        a[p, :8] = np.random.permutation(np.resize(levels, 8))
        for g in range(8):
            far = levels[np.abs(levels - a[p, g]) >= 10]
            a[p, g + 8] = far[np.random.randint(len(far))]
    return np.exp2(a.ravel()).repeat(32)


BF16 = ml_dtypes.bfloat16


def bf(x):
    return np.asarray(x, np.float32).astype(BF16)


def f64(x):
    return np.asarray(x).astype(np.float64)


B, N, D, R, Q = 4, 1024, 1024, 16, 16


def setup_inputs():
    s = mx_kscale(D)
    return {"x": bf(np.random.standard_normal((B, N, D)) * s),
            "w0": bf(np.random.standard_normal((B, N, R))),
            "core1": bf(np.random.standard_normal((R, D, Q)) / np.sqrt(D * R) / s[None, :, None]),
            "core2": bf(np.random.standard_normal((Q, D, R)) / np.sqrt(D * Q) / s[None, :, None])}


def reference(x, w0, core1, core2):
    xq = mxq(f64(x), 2, "e4m3")
    c1 = mxq(f64(core1), 1, "e4m3").transpose(1, 0, 2).reshape(D, R * Q)
    c2 = mxq(f64(core2), 1, "e4m3").transpose(1, 0, 2).reshape(D, Q * R)
    m1 = (xq @ c1).reshape(B, N, R, Q)
    m2 = (xq @ c2).reshape(B, N, Q, R)
    w1 = (f64(w0)[..., :, None] * m1).sum(-2)
    w2 = (w1[..., :, None] * m2).sum(-2)
    return w2

@@ -1,0 +1,260 @@
+from contextlib import ExitStack
+
+import concourse.mybir as mybir
+from concourse.masks import make_identity
+
+F32 = mybir.dt.float32
+BF16 = mybir.dt.bfloat16
+U32 = mybir.dt.uint32
+U8 = mybir.dt.uint8
+FP8X4 = mybir.dt.float8_e4m3fn_x4
+ADD = mybir.AluOpType.add
+MULT = mybir.AluOpType.mult
+AXIS_X = mybir.AxisListType.X
+
+P = 128
+TOKENS = 4096
+D = 1024
+R = 16
+TILES = TOKENS // P
+CH = 4
+NCH = TILES // CH
+FLOPS = 2 * TOKENS * D * 512 + 4 * TOKENS * 256
+
+
+def tile_linear_pa_kernel(tc, x, w0, core1, core2, out):
+    nc = tc.nc
+    xv = x.flatten_outer_dims().rearrange("(p j) d -> p j d", j=TILES)
+    w0v = w0.flatten_outer_dims().rearrange("(p j) r -> p (j r)", j=TILES)
+    outv = out.flatten_outer_dims().rearrange("(p j) r -> p j r", j=TILES)
+
+    with ExitStack() as ctx:
+        keep = ctx.enter_context(tc.tile_pool(name="keep", bufs=1))
+        stage = ctx.enter_context(tc.tile_pool(name="stage", bufs=3))
+        ps_t = ctx.enter_context(tc.psum_pool(name="ps_t", bufs=4))
+        ps_a = ctx.enter_context(tc.psum_pool(name="ps_a", bufs=2))
+        ps_b = ctx.enter_context(tc.psum_pool(name="ps_b", bufs=2))
+        ctx.enter_context(tc.manual_schedule())
+
+        wl = keep.tile([P, 8192], BF16)
+        xs = []
+        xcodes = []
+        xscales = []
+        for c in range(NCH):
+            x_sb = keep.tile([P, CH, D], BF16, name="x_sb%d" % c)
+            xs.append(x_sb)
+            codes = keep.tile([P, CH * 256], U32, align_bytes=64, name="codes%d" % c)
+            xcodes.append(codes)
+            scales = keep.tile([P, CH * 256], U8, align_bytes=64, name="scales%d" % c)
+            xscales.append(scales)
+        for core, (eng, src) in enumerate(((nc.sync, core1), (nc.scalar, core2))):
+            rows = src.rearrange("a (g l) b -> (a g) (l b)", g=2)
+            for u in range(2):
+                eng.dma_start(out=wl[2 * u + core:128:4, 0:8192 - 32 * u], in_=rows[:, 32 * u:8192])
+        w0_sb = keep.tile([P, TILES * R], BF16)
+        nc.scalar.dma_start(out=w0_sb[:], in_=w0v)
+        for c in range(NCH):
+            nc.sync.dma_start(out=xs[c][:], in_=xv[:, c * CH:(c + 1) * CH, :])
+
+        zeros = keep.tile([P, P], F32)
+        nc.vector.memset(zeros[:], 0.0)
+        ident = keep.tile([P, P], F32)
+        make_identity(nc, ident[:])
+
+        def idle_matmuls(bank_columns, count):
+            for i in range(count):
+                nc.tensor.matmul(out=bank_columns, lhsT=zeros[:], rhs=zeros[:], start=True, stop=True)
+        out_sb = keep.tile([P, TILES * R], F32)
+
+        wgrp = keep.tile([P, 2, 2048], BF16, align_bytes=64)
+        wcodes = keep.tile([P, 2, 512], U32, align_bytes=64)
+        wscales = keep.tile([P, 2, 512], U8, align_bytes=64)
+        wd = keep.tile([P, 4096], BF16)
+
+        def weights():
+            wl_v = wl[:].rearrange("p (m v e b) -> p v m e b", v=2, e=2, b=16)[:, 0]
+            for k, eng in ((0, "v"), (2, "s"), (3, "g"), (1, "v")):
+                dst = wd[:, k * 1024:(k + 1) * 1024].rearrange("p (b m e) -> p m e b", b=4, e=2)
+                src = wl_v[:, :, :, 4 * k:4 * k + 4]
+                if eng == "v":
+                    nc.vector.tensor_copy(out=dst, in_=src)
+                elif eng == "s":
+                    nc.scalar.copy(out=dst, in_=src)
+                else:
+                    nc.gpsimd.tensor_scalar(out=dst, in0=src, scalar1=1.0, scalar2=0.0, op0=MULT, op1=ADD)
+            wts = []
+            for k in range(4):
+                pool = ps_a if k < 2 else ps_b
+                wt = pool.tile([P, 512], F32, tag="bank%d" % (k // 2))
+                wts.append(wt)
+                if k == 0:
+                    idle_matmuls(wt[:, 0:P], 16)
+                for bb in range(4):
+                    b = 4 * k + bb
+                    nc.tensor.transpose(
+                        wt[:, bb * P:(bb + 1) * P], wd[:, b * 256:(b + 1) * 256].bitcast(F32), ident[:])
+            words = wgrp[:].rearrange("p g n -> p (g n)").bitcast(F32)
+            dst1 = words.rearrange("p (g c b a u) -> p c g b a u", g=2, c=2, b=16, a=16)[:, 0]
+            dst2 = words.rearrange("p (g c a b u) -> p c g a b u", g=2, c=2, b=16, a=16)[:, 1]
+            for k in range(2):
+                src = wts[k][:].rearrange("p (b a g u c) -> p c g b a u", b=4, c=2, a=16, g=2)
+                nc.vector.tensor_copy(out=dst1[:, :, 4 * k:4 * k + 4], in_=src[:, 0])
+                nc.vector.tensor_copy(
+                    out=dst2[:, :, :, 4 * k:4 * k + 4], in_=src[:, 1].rearrange("p g b a u -> p g a b u"))
+            for g in range(2):
+                for k in range(2, 4):
+                    src = wts[k][:].rearrange("p (b a g u c) -> p c g b a u", b=4, c=2, a=16, g=2)
+                    nc.scalar.copy(out=dst1[:, g, 4 * k:4 * k + 4], in_=src[:, 0, g])
+            quantise_core(0)
+            return wts, dst2
+
+        def quantise_core(core):
+            for g in range(2):
+                nc.vector.quantize_mx(
+                    out=wcodes[:, g, core * 256:(core + 1) * 256].bitcast(FP8X4),
+                    scales=wscales[:, g, core * 256:(core + 1) * 256],
+                    in_=wgrp[:, g, core * 1024:(core + 1) * 1024])
+
+        def weights_core2(wts, dst2):
+            for g in range(2):
+                for k in range(2, 4):
+                    src = wts[k][:].rearrange("p (b a g u c) -> p c g b a u", b=4, c=2, a=16, g=2)
+                    nc.scalar.copy(
+                        out=dst2[:, g, :, 4 * k:4 * k + 4], in_=src[:, 1, g].rearrange("p b a u -> p a b u"))
+            quantise_core(1)
+
+        grouped_of = {}
+        bank_of = {}
+        p1_of = {}
+        p2_of = {}
+        w1_of = {}
+
+        def transposes(c, tiles, on_vector=(), idle_first=0):
+            if c not in grouped_of:
+                new_grouped = stage.tile([P, CH * 1024], BF16, align_bytes=64, tag="grouped")
+                grouped_of[c] = new_grouped
+            grouped = grouped_of[c]
+            for jj in tiles:
+                xt = ps_t.tile([P, 512], F32, tag="xt")
+                xw = xs[c][:, jj, :].bitcast(F32)
+                if jj == tiles[0]:
+                    idle_matmuls(xt[:, 0:P], idle_first)
+                for k in range(4):
+                    first = 256 * (k // 2) + k % 2
+                    nc.tensor.transpose(xt[:, k * P:(k + 1) * P], xw[:, first:256 * (k // 2 + 1):2], ident[:])
+                dst = grouped[:, jj * 1024:(jj + 1) * 1024].bitcast(F32).rearrange(
+                    "p (g r u) -> p g r u", g=2, u=2)
+                src = xt[:].rearrange("p (g u r) -> p g r u", g=2, u=2)
+                if jj in on_vector:
+                    nc.vector.tensor_copy(out=dst, in_=src)
+                else:
+                    nc.scalar.copy(out=dst, in_=src)
+
+        def quantise(c, parts=1):
+            w = CH * 256 // parts
+            for h in range(parts):
+                nc.vector.quantize_mx(
+                    out=xcodes[c][:, h * w:(h + 1) * w].bitcast(FP8X4),
+                    scales=xscales[c][:, h * w:(h + 1) * w],
+                    in_=grouped_of[c][:, 4 * h * w:4 * (h + 1) * w])
+
+        def passes(c, core):
+            pool = ps_a if core == 0 else ps_b
+            for h in range(2):
+                bank = pool.tile([P, 512], F32, tag="bank%d" % core)
+                bank_of[(c, core, h)] = bank
+                for t in range(2):
+                    jj = 2 * h + t
+                    for g in range(2):
+                        cols = slice((jj * 2 + g) * P, (jj * 2 + g + 1) * P)
+                        nc.tensor.matmul_mx(
+                            out=bank[:, t * 256:(t + 1) * 256],
+                            lhsT=xcodes[c][:, cols].bitcast(FP8X4), lhsT_scale=xscales[c][:, cols],
+                            rhs=wcodes[:, g, core * 256:(core + 1) * 256].bitcast(FP8X4),
+                            rhs_scale=wscales[:, g, core * 256:(core + 1) * 256],
+                            start=(g == 0), stop=(g == 1),
+                        )
+
+        def mult_a(c):
+            p1 = stage.tile([P, CH * 256], F32, tag="p1")
+            p1_of[c] = p1
+            for h in range(2):
+                j0 = c * CH + 2 * h
+                nc.vector.tensor_tensor(
+                    out=p1[:, h * 512:(h + 1) * 512].rearrange("p (t q r) -> p t q r", t=2, q=16),
+                    in0=bank_of[(c, 0, h)][:].rearrange("p (t q r) -> p t q r", t=2, q=16),
+                    in1=w0_sb[:, j0 * R:(j0 + 2) * R].rearrange(
+                        "p (t r) -> p t r", t=2).unsqueeze(2).to_broadcast([P, 2, 16, 16]),
+                    op=MULT,
+                )
+
+        def sum_a(c):
+            w1 = stage.tile([P, CH * 16], F32, tag="w1")
+            w1_of[c] = w1
+            nc.vector.tensor_reduce(
+                out=w1[:], in_=p1_of[c][:].rearrange("p (n r) -> p n r", r=16), axis=AXIS_X, op=ADD)
+
+        def mult_b(c):
+            p2 = stage.tile([P, CH, 256], F32, tag="p2")
+            p2_of[c] = p2
+            for h in range(2):
+                w1_h = w1_of[c][:, h * 32:(h + 1) * 32].rearrange("p (t q) -> p t q", t=2)
+                if c == NCH - 1:
+                    nc.vector.tensor_tensor(
+                        out=p2[:, 2 * h:2 * h + 2, :].rearrange("p t (r q) -> p t r q", q=16),
+                        in0=bank_of[(c, 1, h)][:].rearrange("p (t q r) -> p t r q", t=2, q=16),
+                        in1=w1_h.unsqueeze(2).to_broadcast([P, 2, 16, 16]),
+                        op=MULT,
+                    )
+                else:
+                    nc.vector.tensor_tensor(
+                        out=p2[:, 2 * h:2 * h + 2, :].rearrange("p t (q r) -> p t q r", q=16),
+                        in0=bank_of[(c, 1, h)][:].rearrange("p (t q r) -> p t q r", t=2, q=16),
+                        in1=w1_h.unsqueeze(3).to_broadcast([P, 2, 16, 16]),
+                        op=MULT,
+                    )
+
+        def sum_b(c):
+            p2 = p2_of[c]
+            o_view = out_sb[:, c * CH * R:(c + 1) * CH * R].rearrange("p (t r) -> p t r", r=R)
+            if c == NCH - 1:
+                nc.vector.tensor_reduce(
+                    out=o_view, in_=p2[:].rearrange("p t (r q) -> p t r q", q=16), axis=AXIS_X, op=ADD)
+            else:
+                for half in (128, 64, 32):
+                    nc.gpsimd.tensor_tensor(
+                        out=p2[:, :, 0:half], in0=p2[:, :, 0:half], in1=p2[:, :, half:2 * half], op=ADD)
+                nc.gpsimd.tensor_tensor(out=o_view, in0=p2[:, :, 0:16], in1=p2[:, :, 16:32], op=ADD)
+            nc.sync.dma_start(out=outv[:, c * CH:(c + 1) * CH, :], in_=o_view)
+
+        def live(c):
+            return 0 <= c < NCH
+
+        whole = (0, 1, 2, 3)
+        wts_left, dst2_left = weights()
+        transposes(0, whole, on_vector=(3,), idle_first=2)
+        quantise(0, parts=2)
+        weights_core2(wts_left, dst2_left)
+        transposes(1, (0, 1), idle_first=2)
+        passes(0, 0)
+        transposes(1, (2, 3))
+        transposes(2, whole)
+        transposes(3, whole)
+        mult_a(0)
+        sum_a(0)
+        quantise(1)
+        passes(1, 0)
+        for c in range(NCH):
+            if live(c + 2):
+                quantise(c + 2)
+            passes(c, 1)
+            if c > 0:
+                sum_a(c)
+            if live(c + 4):
+                transposes(c + 4, whole)
+            if live(c + 1):
+                mult_a(c + 1)
+            if live(c + 2):
+                passes(c + 2, 0)
+            mult_b(c)
+            sum_b(c)

@@ -58,6 +58,8 @@ def tile_linear_pa_kernel(tc, x, w0, core1, core2, out):
 
         zeros = keep.tile([P, P], F32)
         nc.vector.memset(zeros[:], 0.0)
+        scratch = keep.tile([P, 1], F32)
+        nc.scalar.copy(out=scratch[:], in_=zeros[:, 0:1])
         ident = keep.tile([P, P], F32)
         make_identity(nc, ident[:])
 
@@ -73,15 +75,13 @@ def tile_linear_pa_kernel(tc, x, w0, core1, core2, out):
 
         def weights():
             wl_v = wl[:].rearrange("p (m v e b) -> p v m e b", v=2, e=2, b=16)[:, 0]
-            for k, eng in ((0, "v"), (2, "s"), (3, "g"), (1, "v")):
+            for k, eng in ((0, "v"), (2, "s"), (1, "v"), (3, "v")):
                 dst = wd[:, k * 1024:(k + 1) * 1024].rearrange("p (b m e) -> p m e b", b=4, e=2)
                 src = wl_v[:, :, :, 4 * k:4 * k + 4]
                 if eng == "v":
                     nc.vector.tensor_copy(out=dst, in_=src)
-                elif eng == "s":
-                    nc.scalar.copy(out=dst, in_=src)
                 else:
-                    nc.gpsimd.tensor_scalar(out=dst, in0=src, scalar1=1.0, scalar2=0.0, op0=MULT, op1=ADD)
+                    nc.scalar.copy(out=dst, in_=src)
             wts = []
             for k in range(4):
                 pool = ps_a if k < 2 else ps_b
@@ -235,26 +235,27 @@ def tile_linear_pa_kernel(tc, x, w0, core1, core2, out):
         transposes(0, whole, on_vector=(3,), idle_first=2)
         quantise(0, parts=2)
         weights_core2(wts_left, dst2_left)
-        transposes(1, (0, 1), idle_first=2)
+        transposes(1, whole, idle_first=2)
         passes(0, 0)
-        transposes(1, (2, 3))
+        passes(0, 1)
         transposes(2, whole)
-        transposes(3, whole)
         mult_a(0)
         sum_a(0)
         quantise(1)
         passes(1, 0)
-        for c in range(NCH):
-            if live(c + 2):
-                quantise(c + 2)
+        mult_b(0)
+        sum_b(0)
+        mult_a(1)
+        transposes(3, whole)
+        for c in range(1, NCH):
             passes(c, 1)
-            if c > 0:
-                sum_a(c)
-            if live(c + 4):
-                transposes(c + 4, whole)
+            if live(c + 1):
+                quantise(c + 1)
+                passes(c + 1, 0)
+            sum_a(c)
+            if live(c + 3):
+                transposes(c + 3, whole)
             if live(c + 1):
                 mult_a(c + 1)
-            if live(c + 2):
-                passes(c + 2, 0)
             mult_b(c)
             sum_b(c)

@@ -87,8 +87,7 @@ def tile_linear_pa_kernel(tc, x, w0, core1, core2, out):
                 pool = ps_a if k < 2 else ps_b
                 wt = pool.tile([P, 512], F32, tag="bank%d" % (k // 2))
                 wts.append(wt)
-                if k == 0:
-                    idle_matmuls(wt[:, 0:P], 16)
+                idle_matmuls(wt[:, 0:P], 16 if k == 0 else 1)
                 for bb in range(4):
                     b = 4 * k + bb
                     nc.tensor.transpose(
@@ -129,7 +128,7 @@ def tile_linear_pa_kernel(tc, x, w0, core1, core2, out):
         p2_of = {}
         w1_of = {}
 
-        def transposes(c, tiles, on_vector=(), idle_first=0):
+        def transposes(c, tiles, on_vector=(), idle_each=0):
             if c not in grouped_of:
                 new_grouped = stage.tile([P, CH * 1024], BF16, align_bytes=64, tag="grouped")
                 grouped_of[c] = new_grouped
@@ -137,8 +136,7 @@ def tile_linear_pa_kernel(tc, x, w0, core1, core2, out):
             for jj in tiles:
                 xt = ps_t.tile([P, 512], F32, tag="xt")
                 xw = xs[c][:, jj, :].bitcast(F32)
-                if jj == tiles[0]:
-                    idle_matmuls(xt[:, 0:P], idle_first)
+                idle_matmuls(xt[:, 0:P], idle_each)
                 for k in range(4):
                     first = 256 * (k // 2) + k % 2
                     nc.tensor.transpose(xt[:, k * P:(k + 1) * P], xw[:, first:256 * (k // 2 + 1):2], ident[:])
@@ -232,10 +230,10 @@ def tile_linear_pa_kernel(tc, x, w0, core1, core2, out):
 
         whole = (0, 1, 2, 3)
         wts_left, dst2_left = weights()
-        transposes(0, whole, on_vector=(3,), idle_first=2)
+        transposes(0, whole, on_vector=(3,), idle_each=1)
         quantise(0, parts=2)
         weights_core2(wts_left, dst2_left)
-        transposes(1, whole, idle_first=2)
+        transposes(1, whole, idle_each=1)
         passes(0, 0)
         passes(0, 1)
         transposes(2, whole)

@@ -47,13 +47,16 @@ def tile_linear_pa_kernel(tc, x, w0, core1, core2, out):
             xcodes.append(codes)
             scales = keep.tile([P, CH * 256], U8, align_bytes=64, name="scales%d" % c)
             xscales.append(scales)
-        for core, (eng, src) in enumerate(((nc.sync, core1), (nc.scalar, core2))):
+        nc.sync.dma_start(out=xs[0][:, 0:2, :], in_=xv[:, 0:2, :])
+        nc.sync.dma_start(out=xs[0][:, 2:4, :], in_=xv[:, 2:4, :])
+        nc.sync.dma_start(out=xs[1][:], in_=xv[:, CH:2 * CH, :])
+        for core, src in enumerate((core1, core2)):
             rows = src.rearrange("a (g l) b -> (a g) (l b)", g=2)
             for u in range(2):
-                eng.dma_start(out=wl[2 * u + core:128:4, 0:8192 - 32 * u], in_=rows[:, 32 * u:8192])
+                nc.sync.dma_start(out=wl[2 * u + core:128:4, 0:8192 - 32 * u], in_=rows[:, 32 * u:8192])
         w0_sb = keep.tile([P, TILES * R], BF16)
-        nc.scalar.dma_start(out=w0_sb[:], in_=w0v)
-        for c in range(NCH):
+        nc.sync.dma_start(out=w0_sb[:], in_=w0v)
+        for c in range(2, NCH):
             nc.sync.dma_start(out=xs[c][:], in_=xv[:, c * CH:(c + 1) * CH, :])
 
         zeros = keep.tile([P, P], F32)
@@ -87,7 +90,7 @@ def tile_linear_pa_kernel(tc, x, w0, core1, core2, out):
                 pool = ps_a if k < 2 else ps_b
                 wt = pool.tile([P, 512], F32, tag="bank%d" % (k // 2))
                 wts.append(wt)
-                idle_matmuls(wt[:, 0:P], 16 if k == 0 else 1)
+                idle_matmuls(wt[:, 0:P], 3 if k == 0 else 1)
                 for bb in range(4):
                     b = 4 * k + bb
                     nc.tensor.transpose(
@@ -104,8 +107,13 @@ def tile_linear_pa_kernel(tc, x, w0, core1, core2, out):
                 for k in range(2, 4):
                     src = wts[k][:].rearrange("p (b a g u c) -> p c g b a u", b=4, c=2, a=16, g=2)
                     nc.scalar.copy(out=dst1[:, g, 4 * k:4 * k + 4], in_=src[:, 0, g])
+            for g in range(2):
+                for k in range(2, 4):
+                    src = wts[k][:].rearrange("p (b a g u c) -> p c g b a u", b=4, c=2, a=16, g=2)
+                    nc.scalar.copy(
+                        out=dst2[:, g, :, 4 * k:4 * k + 4], in_=src[:, 1, g].rearrange("p b a u -> p a b u"))
             quantise_core(0)
-            return wts, dst2
+            quantise_core(1)
 
         def quantise_core(core):
             for g in range(2):
@@ -113,14 +121,6 @@ def tile_linear_pa_kernel(tc, x, w0, core1, core2, out):
                     out=wcodes[:, g, core * 256:(core + 1) * 256].bitcast(FP8X4),
                     scales=wscales[:, g, core * 256:(core + 1) * 256],
                     in_=wgrp[:, g, core * 1024:(core + 1) * 1024])
-
-        def weights_core2(wts, dst2):
-            for g in range(2):
-                for k in range(2, 4):
-                    src = wts[k][:].rearrange("p (b a g u c) -> p c g b a u", b=4, c=2, a=16, g=2)
-                    nc.scalar.copy(
-                        out=dst2[:, g, :, 4 * k:4 * k + 4], in_=src[:, 1, g].rearrange("p b a u -> p a b u"))
-            quantise_core(1)
 
         grouped_of = {}
         bank_of = {}
@@ -192,9 +192,20 @@ def tile_linear_pa_kernel(tc, x, w0, core1, core2, out):
             nc.vector.tensor_reduce(
                 out=w1[:], in_=p1_of[c][:].rearrange("p (n r) -> p n r", r=16), axis=AXIS_X, op=ADD)
 
-        def mult_b(c):
+        def scalar_b(c):
             p2 = stage.tile([P, CH, 256], F32, tag="p2")
             p2_of[c] = p2
+            if c == NCH - 1:
+                return
+            for q in range(16):
+                nc.scalar.activation(
+                    out=p2[:, 3, q * 16:(q + 1) * 16],
+                    in_=bank_of[(c, 1, 1)][:, 256 + q * 16:256 + (q + 1) * 16],
+                    func=mybir.ActivationFunctionType.Copy,
+                    scale=w1_of[c][:, 48 + q:49 + q])
+
+        def mult_b(c):
+            p2 = p2_of[c]
             for h in range(2):
                 w1_h = w1_of[c][:, h * 32:(h + 1) * 32].rearrange("p (t q) -> p t q", t=2)
                 if c == NCH - 1:
@@ -205,10 +216,11 @@ def tile_linear_pa_kernel(tc, x, w0, core1, core2, out):
                         op=MULT,
                     )
                 else:
+                    n = 2 - h
                     nc.vector.tensor_tensor(
-                        out=p2[:, 2 * h:2 * h + 2, :].rearrange("p t (q r) -> p t q r", q=16),
-                        in0=bank_of[(c, 1, h)][:].rearrange("p (t q r) -> p t q r", t=2, q=16),
-                        in1=w1_h.unsqueeze(3).to_broadcast([P, 2, 16, 16]),
+                        out=p2[:, 2 * h:2 * h + n, :].rearrange("p t (q r) -> p t q r", q=16),
+                        in0=bank_of[(c, 1, h)][:, 0:n * 256].rearrange("p (t q r) -> p t q r", t=n, q=16),
+                        in1=w1_h[:, 0:n].unsqueeze(3).to_broadcast([P, n, 16, 16]),
                         op=MULT,
                     )
 
@@ -229,28 +241,31 @@ def tile_linear_pa_kernel(tc, x, w0, core1, core2, out):
             return 0 <= c < NCH
 
         whole = (0, 1, 2, 3)
-        wts_left, dst2_left = weights()
-        transposes(0, whole, on_vector=(3,), idle_each=1)
-        quantise(0, parts=2)
-        weights_core2(wts_left, dst2_left)
-        transposes(1, whole, idle_each=1)
+        warm = ps_a.tile([P, 512], F32, tag="bank0")
+        idle_matmuls(warm[:, 0:P], 6)
+        transposes(0, whole, on_vector=(1, 3), idle_each=1)
+        quantise(0)
+        transposes(1, whole, on_vector=(1, 3), idle_each=1)
+        weights()
+        transposes(2, whole)
+        quantise(1)
         passes(0, 0)
         passes(0, 1)
-        transposes(2, whole)
         mult_a(0)
         sum_a(0)
-        quantise(1)
+        scalar_b(0)
         passes(1, 0)
+        transposes(3, whole)
+        mult_a(1)
         mult_b(0)
         sum_b(0)
-        mult_a(1)
-        transposes(3, whole)
         for c in range(1, NCH):
             passes(c, 1)
             if live(c + 1):
                 quantise(c + 1)
                 passes(c + 1, 0)
             sum_a(c)
+            scalar_b(c)
             if live(c + 3):
                 transposes(c + 3, whole)
             if live(c + 1):

@@ -189,8 +189,10 @@ def tile_linear_pa_kernel(tc, x, w0, core1, core2, out):
         def sum_a(c):
             w1 = stage.tile([P, CH * 16], F32, tag="w1")
             w1_of[c] = w1
-            nc.vector.tensor_reduce(
-                out=w1[:], in_=p1_of[c][:].rearrange("p (n r) -> p n r", r=16), axis=AXIS_X, op=ADD)
+            for h in range(2):
+                nc.vector.tensor_reduce(
+                    out=w1[:, h * 32:(h + 1) * 32],
+                    in_=p1_of[c][:, h * 512:(h + 1) * 512].rearrange("p (n r) -> p n r", r=16), axis=AXIS_X, op=ADD)
 
         def scalar_b(c):
             p2 = stage.tile([P, CH, 256], F32, tag="p2")
@@ -249,26 +251,17 @@ def tile_linear_pa_kernel(tc, x, w0, core1, core2, out):
         weights()
         transposes(2, whole)
         quantise(1)
-        passes(0, 0)
-        passes(0, 1)
-        mult_a(0)
-        sum_a(0)
-        scalar_b(0)
-        passes(1, 0)
-        transposes(3, whole)
-        mult_a(1)
-        mult_b(0)
-        sum_b(0)
-        for c in range(1, NCH):
-            passes(c, 1)
-            if live(c + 1):
-                quantise(c + 1)
-                passes(c + 1, 0)
+        for c in range(NCH):
+            passes(c, 0)
+            if live(c + 3):
+                transposes(c + 3, (0, 1))
+            mult_a(c)
             sum_a(c)
+            passes(c, 1)
             scalar_b(c)
             if live(c + 3):
-                transposes(c + 3, whole)
-            if live(c + 1):
-                mult_a(c + 1)
+                transposes(c + 3, (2, 3))
+            if live(c + 2):
+                quantise(c + 2)
             mult_b(c)
             sum_b(c)

@@ -36,7 +36,10 @@ def tile_linear_pa_kernel(tc, x, w0, core1, core2, out):
         ps_b = ctx.enter_context(tc.psum_pool(name="ps_b", bufs=2))
         ctx.enter_context(tc.manual_schedule())
 
-        wl = keep.tile([P, 8192], BF16)
+        wl = []
+        for half in range(2):
+            wl_half = keep.tile([P, 4096], BF16, name="wl%d" % half)
+            wl.append(wl_half)
         xs = []
         xcodes = []
         xscales = []
@@ -50,10 +53,13 @@ def tile_linear_pa_kernel(tc, x, w0, core1, core2, out):
         nc.sync.dma_start(out=xs[0][:, 0:2, :], in_=xv[:, 0:2, :])
         nc.sync.dma_start(out=xs[0][:, 2:4, :], in_=xv[:, 2:4, :])
         nc.sync.dma_start(out=xs[1][:], in_=xv[:, CH:2 * CH, :])
-        for core, src in enumerate((core1, core2)):
-            rows = src.rearrange("a (g l) b -> (a g) (l b)", g=2)
-            for u in range(2):
-                nc.sync.dma_start(out=wl[2 * u + core:128:4, 0:8192 - 32 * u], in_=rows[:, 32 * u:8192])
+        for half, wl_half in enumerate(wl):
+            for core, src in enumerate((core1, core2)):
+                rows = src.rearrange("a (g l) b -> (a g) (l b)", g=2)
+                for u in range(2):
+                    first = half * 4096 + 32 * u
+                    width = min(4096, 8192 - first)
+                    nc.sync.dma_start(out=wl_half[2 * u + core:128:4, 0:width], in_=rows[:, first:first + width])
         w0_sb = keep.tile([P, TILES * R], BF16)
         nc.sync.dma_start(out=w0_sb[:], in_=w0v)
         for c in range(2, NCH):
@@ -77,14 +83,16 @@ def tile_linear_pa_kernel(tc, x, w0, core1, core2, out):
         wd = keep.tile([P, 4096], BF16)
 
         def weights():
-            wl_v = wl[:].rearrange("p (m v e b) -> p v m e b", v=2, e=2, b=16)[:, 0]
-            for k, eng in ((0, "v"), (2, "s"), (1, "v"), (3, "v")):
-                dst = wd[:, k * 1024:(k + 1) * 1024].rearrange("p (b m e) -> p m e b", b=4, e=2)
-                src = wl_v[:, :, :, 4 * k:4 * k + 4]
-                if eng == "v":
-                    nc.vector.tensor_copy(out=dst, in_=src)
-                else:
-                    nc.scalar.copy(out=dst, in_=src)
+            for half in range(2):
+                ms = slice(half * 64, (half + 1) * 64)
+                wl_v = wl[half][:].rearrange("p (m v e b) -> p v m e b", v=2, e=2, b=16)[:, 0]
+                for k, eng in ((0, "v"), (2, "s"), (1, "v"), (3, "v")):
+                    dst = wd[:, k * 1024:(k + 1) * 1024].rearrange("p (b m e) -> p m e b", b=4, e=2)[:, ms]
+                    src = wl_v[:, :, :, 4 * k:4 * k + 4]
+                    if eng == "v":
+                        nc.vector.tensor_copy(out=dst, in_=src)
+                    else:
+                        nc.scalar.copy(out=dst, in_=src)
             wts = []
             for k in range(4):
                 pool = ps_a if k < 2 else ps_b
@@ -128,6 +136,17 @@ def tile_linear_pa_kernel(tc, x, w0, core1, core2, out):
         p2_of = {}
         w1_of = {}
 
+        ordered_of = {}
+
+        def order(c):
+            if not live(c):
+                return
+            ordered = stage.tile([P, 512], F32, tag="ordered")
+            ordered_of[(c, 3)] = ordered
+            nc.scalar.copy(
+                out=ordered[:].rearrange("p (g u r) -> p g u r", g=2, u=2),
+                in_=xs[c][:, 3, :].bitcast(F32).rearrange("p (g r u) -> p g u r", g=2, u=2))
+
         def transposes(c, tiles, on_vector=(), idle_each=0):
             if c not in grouped_of:
                 new_grouped = stage.tile([P, CH * 1024], BF16, align_bytes=64, tag="grouped")
@@ -138,8 +157,11 @@ def tile_linear_pa_kernel(tc, x, w0, core1, core2, out):
                 xw = xs[c][:, jj, :].bitcast(F32)
                 idle_matmuls(xt[:, 0:P], idle_each)
                 for k in range(4):
-                    first = 256 * (k // 2) + k % 2
-                    nc.tensor.transpose(xt[:, k * P:(k + 1) * P], xw[:, first:256 * (k // 2 + 1):2], ident[:])
+                    if (c, jj) in ordered_of:
+                        words = ordered_of[(c, jj)][:, k * P:(k + 1) * P]
+                    else:
+                        words = xw[:, 256 * (k // 2) + k % 2:256 * (k // 2 + 1):2]
+                    nc.tensor.transpose(xt[:, k * P:(k + 1) * P], words, ident[:])
                 dst = grouped[:, jj * 1024:(jj + 1) * 1024].bitcast(F32).rearrange(
                     "p (g r u) -> p g r u", g=2, u=2)
                 src = xt[:].rearrange("p (g u r) -> p g r u", g=2, u=2)
@@ -197,7 +219,7 @@ def tile_linear_pa_kernel(tc, x, w0, core1, core2, out):
         def scalar_b(c):
             p2 = stage.tile([P, CH, 256], F32, tag="p2")
             p2_of[c] = p2
-            if c == NCH - 1:
+            if c >= NCH - 2:
                 return
             for q in range(16):
                 nc.scalar.activation(
@@ -218,7 +240,7 @@ def tile_linear_pa_kernel(tc, x, w0, core1, core2, out):
                         op=MULT,
                     )
                 else:
-                    n = 2 - h
+                    n = 2 if c == NCH - 2 else 2 - h
                     nc.vector.tensor_tensor(
                         out=p2[:, 2 * h:2 * h + n, :].rearrange("p t (q r) -> p t q r", q=16),
                         in0=bank_of[(c, 1, h)][:, 0:n * 256].rearrange("p (t q r) -> p t q r", t=n, q=16),
@@ -247,9 +269,10 @@ def tile_linear_pa_kernel(tc, x, w0, core1, core2, out):
         idle_matmuls(warm[:, 0:P], 6)
         transposes(0, whole, on_vector=(1, 3), idle_each=1)
         quantise(0)
-        transposes(1, whole, on_vector=(1, 3), idle_each=1)
+        transposes(1, whole, idle_each=1)
         weights()
         transposes(2, whole)
+        order(3)
         quantise(1)
         for c in range(NCH):
             passes(c, 0)
@@ -261,6 +284,7 @@ def tile_linear_pa_kernel(tc, x, w0, core1, core2, out):
             scalar_b(c)
             if live(c + 3):
                 transposes(c + 3, (2, 3))
+            order(c + 4)
             if live(c + 2):
                 quantise(c + 2)
             mult_b(c)

@@ -106,20 +106,24 @@ def tile_linear_pa_kernel(tc, x, w0, core1, core2, out):
             words = wgrp[:].rearrange("p g n -> p (g n)").bitcast(F32)
             dst1 = words.rearrange("p (g c b a u) -> p c g b a u", g=2, c=2, b=16, a=16)[:, 0]
             dst2 = words.rearrange("p (g c a b u) -> p c g a b u", g=2, c=2, b=16, a=16)[:, 1]
+            def bank(k, core):
+                return wts[k][:].rearrange("p (b a g u c) -> p c g b a u", b=4, c=2, a=16, g=2)[:, core]
+
+            def copy1(k):
+                nc.vector.tensor_copy(out=dst1[:, :, 4 * k:4 * k + 4], in_=bank(k, 0))
+
+            copy1(0)
+            copy1(1)
             for k in range(2):
-                src = wts[k][:].rearrange("p (b a g u c) -> p c g b a u", b=4, c=2, a=16, g=2)
-                nc.vector.tensor_copy(out=dst1[:, :, 4 * k:4 * k + 4], in_=src[:, 0])
                 nc.vector.tensor_copy(
-                    out=dst2[:, :, :, 4 * k:4 * k + 4], in_=src[:, 1].rearrange("p g b a u -> p g a b u"))
+                    out=dst2[:, :, :, 4 * k:4 * k + 4], in_=bank(k, 1).rearrange("p g b a u -> p g a b u"))
+            copy1(2)
             for g in range(2):
-                for k in range(2, 4):
-                    src = wts[k][:].rearrange("p (b a g u c) -> p c g b a u", b=4, c=2, a=16, g=2)
-                    nc.scalar.copy(out=dst1[:, g, 4 * k:4 * k + 4], in_=src[:, 0, g])
-            for g in range(2):
-                for k in range(2, 4):
-                    src = wts[k][:].rearrange("p (b a g u c) -> p c g b a u", b=4, c=2, a=16, g=2)
+                nc.scalar.copy(out=dst1[:, g, 12:16], in_=bank(3, 0)[:, g])
+            for k in range(2, 4):
+                for g in range(2):
                     nc.scalar.copy(
-                        out=dst2[:, g, :, 4 * k:4 * k + 4], in_=src[:, 1, g].rearrange("p b a u -> p a b u"))
+                        out=dst2[:, g, :, 4 * k:4 * k + 4], in_=bank(k, 1)[:, g].rearrange("p b a u -> p a b u"))
             quantise_core(0)
             quantise_core(1)
 
@@ -146,6 +150,10 @@ def tile_linear_pa_kernel(tc, x, w0, core1, core2, out):
             nc.scalar.copy(
                 out=ordered[:].rearrange("p (g u r) -> p g u r", g=2, u=2),
                 in_=xs[c][:, 3, :].bitcast(F32).rearrange("p (g r u) -> p g u r", g=2, u=2))
+
+        def idle_in_spare_bank(count):
+            spare = ps_t.tile([P, 512], F32, tag="xt")
+            idle_matmuls(spare[:, 0:P], count)
 
         def transposes(c, tiles, on_vector=(), idle_each=0):
             if c not in grouped_of:
@@ -228,9 +236,9 @@ def tile_linear_pa_kernel(tc, x, w0, core1, core2, out):
                     func=mybir.ActivationFunctionType.Copy,
                     scale=w1_of[c][:, 48 + q:49 + q])
 
-        def mult_b(c):
+        def mult_b(c, halves):
             p2 = p2_of[c]
-            for h in range(2):
+            for h in halves:
                 w1_h = w1_of[c][:, h * 32:(h + 1) * 32].rearrange("p (t q) -> p t q", t=2)
                 if c == NCH - 1:
                     nc.vector.tensor_tensor(
@@ -271,21 +279,27 @@ def tile_linear_pa_kernel(tc, x, w0, core1, core2, out):
         quantise(0)
         transposes(1, whole, idle_each=1)
         weights()
-        transposes(2, whole)
+        transposes(2, (0, 1))
+        transposes(2, (2, 3), idle_each=1)
         order(3)
         quantise(1)
         for c in range(NCH):
+            if c > NCH - 3:
+                idle_in_spare_bank(2)
             passes(c, 0)
             if live(c + 3):
                 transposes(c + 3, (0, 1))
             mult_a(c)
             sum_a(c)
+            if not live(c + 3):
+                idle_in_spare_bank(2)
             passes(c, 1)
             scalar_b(c)
             if live(c + 3):
                 transposes(c + 3, (2, 3))
             order(c + 4)
+            mult_b(c, (0,))
             if live(c + 2):
                 quantise(c + 2)
-            mult_b(c)
+            mult_b(c, (1,))
             sum_b(c)

@@ -89,7 +89,7 @@ def tile_linear_pa_kernel(tc, x, w0, core1, core2, out):
                 for k, eng in ((0, "v"), (2, "s"), (1, "v"), (3, "v")):
                     dst = wd[:, k * 1024:(k + 1) * 1024].rearrange("p (b m e) -> p m e b", b=4, e=2)[:, ms]
                     src = wl_v[:, :, :, 4 * k:4 * k + 4]
-                    if eng == "v":
+                    if eng == "v" or half == 0:
                         nc.vector.tensor_copy(out=dst, in_=src)
                     else:
                         nc.scalar.copy(out=dst, in_=src)
@@ -98,7 +98,7 @@ def tile_linear_pa_kernel(tc, x, w0, core1, core2, out):
                 pool = ps_a if k < 2 else ps_b
                 wt = pool.tile([P, 512], F32, tag="bank%d" % (k // 2))
                 wts.append(wt)
-                idle_matmuls(wt[:, 0:P], 3 if k == 0 else 1)
+                idle_matmuls(wt[:, 0:P], (3, 1, 0, 0)[k])
                 for bb in range(4):
                     b = 4 * k + bb
                     nc.tensor.transpose(
@@ -114,13 +114,11 @@ def tile_linear_pa_kernel(tc, x, w0, core1, core2, out):
 
             copy1(0)
             copy1(1)
-            for k in range(2):
-                nc.vector.tensor_copy(
-                    out=dst2[:, :, :, 4 * k:4 * k + 4], in_=bank(k, 1).rearrange("p g b a u -> p g a b u"))
+            nc.vector.tensor_copy(out=dst2[:, :, :, 0:4], in_=bank(0, 1).rearrange("p g b a u -> p g a b u"))
             copy1(2)
             for g in range(2):
                 nc.scalar.copy(out=dst1[:, g, 12:16], in_=bank(3, 0)[:, g])
-            for k in range(2, 4):
+            for k in range(1, 4):
                 for g in range(2):
                     nc.scalar.copy(
                         out=dst2[:, g, :, 4 * k:4 * k + 4], in_=bank(k, 1)[:, g].rearrange("p b a u -> p a b u"))
@@ -279,25 +277,23 @@ def tile_linear_pa_kernel(tc, x, w0, core1, core2, out):
         quantise(0)
         transposes(1, whole, idle_each=1)
         weights()
-        transposes(2, (0, 1))
-        transposes(2, (2, 3), idle_each=1)
-        order(3)
+        transposes(2, (0, 1), idle_each=1)
         quantise(1)
         for c in range(NCH):
-            if c > NCH - 3:
+            if not live(c + 2):
                 idle_in_spare_bank(2)
             passes(c, 0)
-            if live(c + 3):
-                transposes(c + 3, (0, 1))
+            if live(c + 2):
+                transposes(c + 2, (2, 3))
+            order(c + 3)
             mult_a(c)
             sum_a(c)
-            if not live(c + 3):
+            if not live(c + 2):
                 idle_in_spare_bank(2)
             passes(c, 1)
             scalar_b(c)
             if live(c + 3):
-                transposes(c + 3, (2, 3))
-            order(c + 4)
+                transposes(c + 3, (0, 1))
             mult_b(c, (0,))
             if live(c + 2):
                 quantise(c + 2)

@@ -60,9 +60,11 @@ def tile_linear_pa_kernel(tc, x, w0, core1, core2, out):
                     first = half * 4096 + 32 * u
                     width = min(4096, 8192 - first)
                     nc.sync.dma_start(out=wl_half[2 * u + core:128:4, 0:width], in_=rows[:, first:first + width])
+        nc.sync.dma_start(out=xs[2][:, 0:2, :], in_=xv[:, 2 * CH:2 * CH + 2, :])
         w0_sb = keep.tile([P, TILES * R], BF16)
         nc.sync.dma_start(out=w0_sb[:], in_=w0v)
-        for c in range(2, NCH):
+        nc.sync.dma_start(out=xs[2][:, 2:4, :], in_=xv[:, 2 * CH + 2:3 * CH, :])
+        for c in range(3, NCH):
             nc.sync.dma_start(out=xs[c][:], in_=xv[:, c * CH:(c + 1) * CH, :])
 
         zeros = keep.tile([P, P], F32)
@@ -86,10 +88,10 @@ def tile_linear_pa_kernel(tc, x, w0, core1, core2, out):
             for half in range(2):
                 ms = slice(half * 64, (half + 1) * 64)
                 wl_v = wl[half][:].rearrange("p (m v e b) -> p v m e b", v=2, e=2, b=16)[:, 0]
-                for k, eng in ((0, "v"), (2, "s"), (1, "v"), (3, "v")):
+                for k in (0, 2, 1, 3):
                     dst = wd[:, k * 1024:(k + 1) * 1024].rearrange("p (b m e) -> p m e b", b=4, e=2)[:, ms]
                     src = wl_v[:, :, :, 4 * k:4 * k + 4]
-                    if eng == "v" or half == 0:
+                    if half == 0 or k < 2:
                         nc.vector.tensor_copy(out=dst, in_=src)
                     else:
                         nc.scalar.copy(out=dst, in_=src)
@@ -114,16 +116,14 @@ def tile_linear_pa_kernel(tc, x, w0, core1, core2, out):
 
             copy1(0)
             copy1(1)
-            nc.vector.tensor_copy(out=dst2[:, :, :, 0:4], in_=bank(0, 1).rearrange("p g b a u -> p g a b u"))
             copy1(2)
             for g in range(2):
                 nc.scalar.copy(out=dst1[:, g, 12:16], in_=bank(3, 0)[:, g])
-            for k in range(1, 4):
+            for k in range(4):
                 for g in range(2):
                     nc.scalar.copy(
                         out=dst2[:, g, :, 4 * k:4 * k + 4], in_=bank(k, 1)[:, g].rearrange("p b a u -> p a b u"))
             quantise_core(0)
-            quantise_core(1)
 
         def quantise_core(core):
             for g in range(2):
@@ -258,14 +258,16 @@ def tile_linear_pa_kernel(tc, x, w0, core1, core2, out):
             p2 = p2_of[c]
             o_view = out_sb[:, c * CH * R:(c + 1) * CH * R].rearrange("p (t r) -> p t r", r=R)
             if c == NCH - 1:
-                nc.vector.tensor_reduce(
-                    out=o_view, in_=p2[:].rearrange("p t (r q) -> p t r q", q=16), axis=AXIS_X, op=ADD)
+                for ts in (slice(0, 2), slice(2, 4)):
+                    nc.vector.tensor_reduce(
+                        out=o_view[:, ts], in_=p2[:, ts].rearrange("p t (r q) -> p t r q", q=16), axis=AXIS_X, op=ADD)
+                    nc.sync.dma_start(out=outv[:, c * CH + ts.start:c * CH + ts.stop, :], in_=o_view[:, ts])
             else:
                 for half in (128, 64, 32):
                     nc.gpsimd.tensor_tensor(
                         out=p2[:, :, 0:half], in0=p2[:, :, 0:half], in1=p2[:, :, half:2 * half], op=ADD)
                 nc.gpsimd.tensor_tensor(out=o_view, in0=p2[:, :, 0:16], in1=p2[:, :, 16:32], op=ADD)
-            nc.sync.dma_start(out=outv[:, c * CH:(c + 1) * CH, :], in_=o_view)
+                nc.sync.dma_start(out=outv[:, c * CH:(c + 1) * CH, :], in_=o_view)
 
         def live(c):
             return 0 <= c < NCH
@@ -279,6 +281,7 @@ def tile_linear_pa_kernel(tc, x, w0, core1, core2, out):
         weights()
         transposes(2, (0, 1), idle_each=1)
         quantise(1)
+        quantise_core(1)
         for c in range(NCH):
             if not live(c + 2):
                 idle_in_spare_bank(2)

from contextlib import ExitStack

import concourse.mybir as mybir
from concourse.masks import make_identity

F32 = mybir.dt.float32
BF16 = mybir.dt.bfloat16
U32 = mybir.dt.uint32
U8 = mybir.dt.uint8
FP8X4 = mybir.dt.float8_e4m3fn_x4
ADD = mybir.AluOpType.add
MULT = mybir.AluOpType.mult
AXIS_X = mybir.AxisListType.X

P = 128
TOKENS = 4096
D = 1024
R = 16
TILES = TOKENS // P
CH = 4
NCH = TILES // CH
FLOPS = 2 * TOKENS * D * 512 + 4 * TOKENS * 256


def tile_linear_pa_kernel(tc, x, w0, core1, core2, out):
    nc = tc.nc
    xv = x.flatten_outer_dims().rearrange("(p j) d -> p j d", j=TILES)
    w0v = w0.flatten_outer_dims().rearrange("(p j) r -> p (j r)", j=TILES)
    outv = out.flatten_outer_dims().rearrange("(p j) r -> p j r", j=TILES)

    with ExitStack() as ctx:
        keep = ctx.enter_context(tc.tile_pool(name="keep", bufs=1))
        stage = ctx.enter_context(tc.tile_pool(name="stage", bufs=3))
        ps_t = ctx.enter_context(tc.psum_pool(name="ps_t", bufs=4))
        ps_a = ctx.enter_context(tc.psum_pool(name="ps_a", bufs=2))
        ps_b = ctx.enter_context(tc.psum_pool(name="ps_b", bufs=2))
        ctx.enter_context(tc.manual_schedule())

        wl = []
        for half in range(2):
            wl_half = keep.tile([P, 4096], BF16, name="wl%d" % half)
            wl.append(wl_half)
        xs = []
        xcodes = []
        xscales = []
        for c in range(NCH):
            x_sb = keep.tile([P, CH, D], BF16, name="x_sb%d" % c)
            xs.append(x_sb)
            codes = keep.tile([P, CH * 256], U32, align_bytes=64, name="codes%d" % c)
            xcodes.append(codes)
            scales = keep.tile([P, CH * 256], U8, align_bytes=64, name="scales%d" % c)
            xscales.append(scales)
        nc.sync.dma_start(out=xs[0][:, 0:2, :], in_=xv[:, 0:2, :])
        nc.sync.dma_start(out=xs[0][:, 2:4, :], in_=xv[:, 2:4, :])
        nc.sync.dma_start(out=xs[1][:], in_=xv[:, CH:2 * CH, :])
        for half, wl_half in enumerate(wl):
            for core, src in enumerate((core1, core2)):
                rows = src.rearrange("a (g l) b -> (a g) (l b)", g=2)
                for u in range(2):
                    first = half * 4096 + 32 * u
                    width = min(4096, 8192 - first)
                    nc.sync.dma_start(out=wl_half[2 * u + core:128:4, 0:width], in_=rows[:, first:first + width])
        nc.sync.dma_start(out=xs[2][:, 0:2, :], in_=xv[:, 2 * CH:2 * CH + 2, :])
        w0_sb = keep.tile([P, TILES * R], BF16)
        nc.sync.dma_start(out=w0_sb[:], in_=w0v)
        nc.sync.dma_start(out=xs[2][:, 2:4, :], in_=xv[:, 2 * CH + 2:3 * CH, :])
        for c in range(3, NCH):
            nc.sync.dma_start(out=xs[c][:], in_=xv[:, c * CH:(c + 1) * CH, :])

        zeros = keep.tile([P, P], F32)
        nc.vector.memset(zeros[:], 0.0)
        scratch = keep.tile([P, 1], F32)
        nc.scalar.copy(out=scratch[:], in_=zeros[:, 0:1])
        ident = keep.tile([P, P], F32)
        make_identity(nc, ident[:])

        def idle_matmuls(bank_columns, count):
            for i in range(count):
                nc.tensor.matmul(out=bank_columns, lhsT=zeros[:], rhs=zeros[:], start=True, stop=True)
        out_sb = keep.tile([P, TILES * R], F32)

        wgrp = keep.tile([P, 2, 2048], BF16, align_bytes=64)
        wcodes = keep.tile([P, 2, 512], U32, align_bytes=64)
        wscales = keep.tile([P, 2, 512], U8, align_bytes=64)
        wd = keep.tile([P, 4096], BF16)

        def weights():
            for half in range(2):
                ms = slice(half * 64, (half + 1) * 64)
                wl_v = wl[half][:].rearrange("p (m v e b) -> p v m e b", v=2, e=2, b=16)[:, 0]
                for k in (0, 2, 1, 3):
                    dst = wd[:, k * 1024:(k + 1) * 1024].rearrange("p (b m e) -> p m e b", b=4, e=2)[:, ms]
                    src = wl_v[:, :, :, 4 * k:4 * k + 4]
                    if half == 0 or k < 2:
                        nc.vector.tensor_copy(out=dst, in_=src)
                    else:
                        nc.scalar.copy(out=dst, in_=src)
            wts = []
            for k in range(4):
                pool = ps_a if k < 2 else ps_b
                wt = pool.tile([P, 512], F32, tag="bank%d" % (k // 2))
                wts.append(wt)
                idle_matmuls(wt[:, 0:P], (3, 1, 0, 0)[k])
                for bb in range(4):
                    b = 4 * k + bb
                    nc.tensor.transpose(
                        wt[:, bb * P:(bb + 1) * P], wd[:, b * 256:(b + 1) * 256].bitcast(F32), ident[:])
            words = wgrp[:].rearrange("p g n -> p (g n)").bitcast(F32)
            dst1 = words.rearrange("p (g c b a u) -> p c g b a u", g=2, c=2, b=16, a=16)[:, 0]
            dst2 = words.rearrange("p (g c a b u) -> p c g a b u", g=2, c=2, b=16, a=16)[:, 1]
            def bank(k, core):
                return wts[k][:].rearrange("p (b a g u c) -> p c g b a u", b=4, c=2, a=16, g=2)[:, core]

            def copy1(k):
                nc.vector.tensor_copy(out=dst1[:, :, 4 * k:4 * k + 4], in_=bank(k, 0))

            copy1(0)
            copy1(1)
            copy1(2)
            for g in range(2):
                nc.scalar.copy(out=dst1[:, g, 12:16], in_=bank(3, 0)[:, g])
            for k in range(4):
                for g in range(2):
                    nc.scalar.copy(
                        out=dst2[:, g, :, 4 * k:4 * k + 4], in_=bank(k, 1)[:, g].rearrange("p b a u -> p a b u"))
            quantise_core(0)

        def quantise_core(core):
            for g in range(2):
                nc.vector.quantize_mx(
                    out=wcodes[:, g, core * 256:(core + 1) * 256].bitcast(FP8X4),
                    scales=wscales[:, g, core * 256:(core + 1) * 256],
                    in_=wgrp[:, g, core * 1024:(core + 1) * 1024])

        grouped_of = {}
        bank_of = {}
        p1_of = {}
        p2_of = {}
        w1_of = {}

        ordered_of = {}

        def order(c):
            if not live(c):
                return
            ordered = stage.tile([P, 512], F32, tag="ordered")
            ordered_of[(c, 3)] = ordered
            nc.scalar.copy(
                out=ordered[:].rearrange("p (g u r) -> p g u r", g=2, u=2),
                in_=xs[c][:, 3, :].bitcast(F32).rearrange("p (g r u) -> p g u r", g=2, u=2))

        def idle_in_spare_bank(count):
            spare = ps_t.tile([P, 512], F32, tag="xt")
            idle_matmuls(spare[:, 0:P], count)

        def transposes(c, tiles, on_vector=(), idle_each=0):
            if c not in grouped_of:
                new_grouped = stage.tile([P, CH * 1024], BF16, align_bytes=64, tag="grouped")
                grouped_of[c] = new_grouped
            grouped = grouped_of[c]
            for jj in tiles:
                xt = ps_t.tile([P, 512], F32, tag="xt")
                xw = xs[c][:, jj, :].bitcast(F32)
                idle_matmuls(xt[:, 0:P], idle_each)
                for k in range(4):
                    if (c, jj) in ordered_of:
                        words = ordered_of[(c, jj)][:, k * P:(k + 1) * P]
                    else:
                        words = xw[:, 256 * (k // 2) + k % 2:256 * (k // 2 + 1):2]
                    nc.tensor.transpose(xt[:, k * P:(k + 1) * P], words, ident[:])
                dst = grouped[:, jj * 1024:(jj + 1) * 1024].bitcast(F32).rearrange(
                    "p (g r u) -> p g r u", g=2, u=2)
                src = xt[:].rearrange("p (g u r) -> p g r u", g=2, u=2)
                if jj in on_vector:
                    nc.vector.tensor_copy(out=dst, in_=src)
                else:
                    nc.scalar.copy(out=dst, in_=src)

        def quantise(c, parts=1):
            w = CH * 256 // parts
            for h in range(parts):
                nc.vector.quantize_mx(
                    out=xcodes[c][:, h * w:(h + 1) * w].bitcast(FP8X4),
                    scales=xscales[c][:, h * w:(h + 1) * w],
                    in_=grouped_of[c][:, 4 * h * w:4 * (h + 1) * w])

        def passes(c, core):
            pool = ps_a if core == 0 else ps_b
            for h in range(2):
                bank = pool.tile([P, 512], F32, tag="bank%d" % core)
                bank_of[(c, core, h)] = bank
                for t in range(2):
                    jj = 2 * h + t
                    for g in range(2):
                        cols = slice((jj * 2 + g) * P, (jj * 2 + g + 1) * P)
                        nc.tensor.matmul_mx(
                            out=bank[:, t * 256:(t + 1) * 256],
                            lhsT=xcodes[c][:, cols].bitcast(FP8X4), lhsT_scale=xscales[c][:, cols],
                            rhs=wcodes[:, g, core * 256:(core + 1) * 256].bitcast(FP8X4),
                            rhs_scale=wscales[:, g, core * 256:(core + 1) * 256],
                            start=(g == 0), stop=(g == 1),
                        )

        def mult_a(c):
            p1 = stage.tile([P, CH * 256], F32, tag="p1")
            p1_of[c] = p1
            for h in range(2):
                j0 = c * CH + 2 * h
                nc.vector.tensor_tensor(
                    out=p1[:, h * 512:(h + 1) * 512].rearrange("p (t q r) -> p t q r", t=2, q=16),
                    in0=bank_of[(c, 0, h)][:].rearrange("p (t q r) -> p t q r", t=2, q=16),
                    in1=w0_sb[:, j0 * R:(j0 + 2) * R].rearrange(
                        "p (t r) -> p t r", t=2).unsqueeze(2).to_broadcast([P, 2, 16, 16]),
                    op=MULT,
                )

        def sum_a(c):
            w1 = stage.tile([P, CH * 16], F32, tag="w1")
            w1_of[c] = w1
            for h in range(2):
                nc.vector.tensor_reduce(
                    out=w1[:, h * 32:(h + 1) * 32],
                    in_=p1_of[c][:, h * 512:(h + 1) * 512].rearrange("p (n r) -> p n r", r=16), axis=AXIS_X, op=ADD)

        def scalar_b(c):
            p2 = stage.tile([P, CH, 256], F32, tag="p2")
            p2_of[c] = p2
            if c >= NCH - 2:
                return
            for q in range(16):
                nc.scalar.activation(
                    out=p2[:, 3, q * 16:(q + 1) * 16],
                    in_=bank_of[(c, 1, 1)][:, 256 + q * 16:256 + (q + 1) * 16],
                    func=mybir.ActivationFunctionType.Copy,
                    scale=w1_of[c][:, 48 + q:49 + q])

        def mult_b(c, halves):
            p2 = p2_of[c]
            for h in halves:
                w1_h = w1_of[c][:, h * 32:(h + 1) * 32].rearrange("p (t q) -> p t q", t=2)
                if c == NCH - 1:
                    nc.vector.tensor_tensor(
                        out=p2[:, 2 * h:2 * h + 2, :].rearrange("p t (r q) -> p t r q", q=16),
                        in0=bank_of[(c, 1, h)][:].rearrange("p (t q r) -> p t r q", t=2, q=16),
                        in1=w1_h.unsqueeze(2).to_broadcast([P, 2, 16, 16]),
                        op=MULT,
                    )
                else:
                    n = 2 if c == NCH - 2 else 2 - h
                    nc.vector.tensor_tensor(
                        out=p2[:, 2 * h:2 * h + n, :].rearrange("p t (q r) -> p t q r", q=16),
                        in0=bank_of[(c, 1, h)][:, 0:n * 256].rearrange("p (t q r) -> p t q r", t=n, q=16),
                        in1=w1_h[:, 0:n].unsqueeze(3).to_broadcast([P, n, 16, 16]),
                        op=MULT,
                    )

        def sum_b(c):
            p2 = p2_of[c]
            o_view = out_sb[:, c * CH * R:(c + 1) * CH * R].rearrange("p (t r) -> p t r", r=R)
            if c == NCH - 1:
                for ts in (slice(0, 2), slice(2, 4)):
                    nc.vector.tensor_reduce(
                        out=o_view[:, ts], in_=p2[:, ts].rearrange("p t (r q) -> p t r q", q=16), axis=AXIS_X, op=ADD)
                    nc.sync.dma_start(out=outv[:, c * CH + ts.start:c * CH + ts.stop, :], in_=o_view[:, ts])
            else:
                for half in (128, 64, 32):
                    nc.gpsimd.tensor_tensor(
                        out=p2[:, :, 0:half], in0=p2[:, :, 0:half], in1=p2[:, :, half:2 * half], op=ADD)
                nc.gpsimd.tensor_tensor(out=o_view, in0=p2[:, :, 0:16], in1=p2[:, :, 16:32], op=ADD)
                nc.sync.dma_start(out=outv[:, c * CH:(c + 1) * CH, :], in_=o_view)

        def live(c):
            return 0 <= c < NCH

        whole = (0, 1, 2, 3)
        warm = ps_a.tile([P, 512], F32, tag="bank0")
        idle_matmuls(warm[:, 0:P], 6)
        transposes(0, whole, on_vector=(1, 3), idle_each=1)
        quantise(0)
        transposes(1, whole, idle_each=1)
        weights()
        transposes(2, (0, 1), idle_each=1)
        quantise(1)
        quantise_core(1)
        for c in range(NCH):
            if not live(c + 2):
                idle_in_spare_bank(2)
            passes(c, 0)
            if live(c + 2):
                transposes(c + 2, (2, 3))
            order(c + 3)
            mult_a(c)
            sum_a(c)
            if not live(c + 2):
                idle_in_spare_bank(2)
            passes(c, 1)
            scalar_b(c)
            if live(c + 3):
                transposes(c + 3, (0, 1))
            mult_b(c, (0,))
            if live(c + 2):
                quantise(c + 2)
            mult_b(c, (1,))
            sum_b(c)
